import numpy as np
import ml_dtypes


def mxq(x, axis, fmt="e4m3"):
    dtype, down = {"e4m3": (ml_dtypes.float8_e4m3fn, 7), "e5m2": (ml_dtypes.float8_e5m2, 14)}[fmt]
    v = np.moveaxis(np.asarray(x, np.float32).astype(ml_dtypes.bfloat16).astype(np.float64), axis, -1)
    blocks = v.reshape(v.shape[:-1] + (-1, 32))
    amax = np.abs(blocks).max(-1, keepdims=True)
    byte = np.maximum(np.where(amax > 0, np.frexp(amax)[1] - 1 + 127, 0) - down, 1)
    scale = np.exp2(byte - 127.0)
    codes = (blocks / scale).astype(np.float32).astype(dtype).astype(np.float64)
    return np.moveaxis((codes * scale).reshape(v.shape), -1, axis)


WIDE = False


def mx_kscale(k):
    if not WIDE:
        return np.ones(k)
    levels = np.array([10, -10, 5, -5, 0])
    if k % 512:
        return np.exp2(np.random.permutation(np.resize(levels, k // 32))).repeat(32)
    a = np.empty((k // 512, 16))
    for p in range(k // 512):
        a[p, :8] = np.random.permutation(np.resize(levels, 8))
        for g in range(8):
            far = levels[np.abs(levels - a[p, g]) >= 10]
            a[p, g + 8] = far[np.random.randint(len(far))]
    return np.exp2(a.ravel()).repeat(32)


BF16 = ml_dtypes.bfloat16


def bf(x):
    return np.asarray(x, np.float32).astype(BF16)


def f64(x):
    return np.asarray(x).astype(np.float64)


B, P0, P1, P2, K0, K1, K2 = 128, 4096, 9216, 7168, 512, 512, 512
PT = P0 + P1 + P2
KT = K0 + K1 + K2
CLIP1 = 1.0


def clip_rows(mat, clip):
    norms = np.sqrt(np.sum(mat * mat, axis=1, keepdims=True))
    scale = np.minimum(clip / norms, 1.0)
    return mat * scale


def setup_inputs():
    t0, t1, t2 = mx_kscale(K0), mx_kscale(K1), mx_kscale(K2)
    r = np.exp2(np.random.uniform(-2.0, 2.0, (B, 1))) / (KT * PT) ** 0.25
    return {"target_grad": bf(np.random.standard_normal((B, PT)) * r),
            "embedding": bf(np.random.standard_normal((B, KT)) * r * np.concatenate([t0, t1, t2])),
            "bases0": bf(np.random.standard_normal((P0, K0)) / np.sqrt(P0) / t0[None, :]),
            "bases1": bf(np.random.standard_normal((P1, K1)) / np.sqrt(P1) / t1[None, :]),
            "bases2": bf(np.random.standard_normal((P2, K2)) / np.sqrt(P2) / t2[None, :])}


def reference(target_grad, embedding, bases0, bases1, bases2):
    g = f64(target_grad)
    e = f64(embedding)
    approx_parts = []
    offset = 0
    for b in (f64(bases0), f64(bases1), f64(bases2)):
        num_k = b.shape[1]
        approx_parts.append(mxq(e[:, offset:offset + num_k], 1, "e4m3") @ mxq(b.T, 0, "e4m3"))
        offset += num_k
    no_reduction_approx = np.concatenate(approx_parts, axis=1)
    residual = g - no_reduction_approx
    return np.sum(clip_rows(residual, CLIP1), axis=0) / B

@@ -1,0 +1,261 @@
+from contextlib import ExitStack
+
+import concourse.mybir as mybir
+from concourse.masks import make_identity
+
+F32 = mybir.dt.float32
+BF16 = mybir.dt.bfloat16
+U32 = mybir.dt.uint32
+U8 = mybir.dt.uint8
+FP8X4 = mybir.dt.float8_e4m3fn_x4
+ALU = mybir.AluOpType
+ACT = mybir.ActivationFunctionType
+
+P = 128
+K = 512
+PACK = 4
+HALVES = 2
+SLOTS = 4
+CHUNK = P * SLOTS
+SLOTS_PER_BANK = 2
+ROUND = 2
+G_ROUNDS = 2
+AHEAD = 3
+TILES_PER_BANK = 4
+PERIOD = 5
+LEAD = 3
+
+FLOPS = 2 * 128 * 20480 * 512
+
+
+def tile_gep_pb_kernel(tc, target_grad, embedding, bases0, bases1, bases2, out):
+    nc = tc.nc
+    groups = (bases0, bases1, bases2)
+    n_groups = len(groups)
+
+    chunk_group = []
+    chunk_rows = []
+    for i, bases in enumerate(groups):
+        for first in range(0, bases.shape[0], CHUNK):
+            chunk_group.append(i)
+            chunk_rows.append(bases[first : first + CHUNK, :])
+    n_rounds = len(chunk_rows) // ROUND
+    round_cols = ROUND * CHUNK
+    n_col_tiles = n_rounds * round_cols // P
+
+    with ExitStack() as stack:
+        keep = stack.enter_context(tc.tile_pool(name="keep", bufs=1))
+        raw_pool = stack.enter_context(tc.tile_pool(name="raw_pool", bufs=(AHEAD + 1) * ROUND))
+        stage = stack.enter_context(tc.tile_pool(name="stage", bufs=2 * ROUND))
+        xt_pool = stack.enter_context(tc.psum_pool(name="xt_pool", bufs=6))
+        acc_pool = stack.enter_context(tc.psum_pool(name="acc_pool", bufs=ROUND))
+        stack.enter_context(tc.manual_schedule())
+
+        ident = keep.tile([P, P], F32, name="ident")
+        e_sb = keep.tile([P, n_groups, K], BF16, name="e_sb")
+        e_grouped = keep.tile([P, n_groups * P * PACK], BF16, name="e_grouped", align_bytes=64)
+        e_codes = keep.tile([P, n_groups, P], U32, name="e_codes", align_bytes=64)
+        e_scales = keep.tile([P, n_groups, P], U8, name="e_scales", align_bytes=64)
+        g_tiles = [
+            keep.tile([P, G_ROUNDS * round_cols], BF16, name="g%d" % q)
+            for q in range(n_rounds // G_ROUNDS)
+        ]
+        r_tiles = [keep.tile([P, round_cols], F32, name="r%d" % n) for n in range(n_rounds)]
+        sq_sums = keep.tile([P, n_rounds], F32, name="sq_sums")
+        one = keep.tile([P, 1], F32, name="one")
+        warm = keep.tile([P, 1], F32, name="warm")
+        norm_sq = keep.tile([P, 1], F32, name="norm_sq")
+        floored = keep.tile([P, 1], F32, name="floored")
+        norm_b = keep.tile([P, 1], F32, name="norm_b")
+        c_over_b = keep.tile([P, 1], F32, name="c_over_b")
+        out_cols = keep.tile([P, 2 * P], F32, name="out_cols")
+        out_rows = keep.tile([P, 2 * P], F32, name="out_rows")
+
+        raw = {}
+        grouped = {}
+        codes = {}
+        scales = {}
+        acc = {}
+
+        def load_round(n):
+            for c in range(n * ROUND, (n + 1) * ROUND):
+                raw[c] = raw_pool.tile([P, SLOTS, K], BF16, name="raw")
+                nc.sync.dma_start(
+                    out=raw[c][:], in_=chunk_rows[c].rearrange("(p t) k -> p t k", t=SLOTS)
+                )
+
+        def load_grad(n):
+            if n % G_ROUNDS == 0:
+                q = n // G_ROUNDS
+                width = G_ROUNDS * round_cols
+                nc.sync.dma_start(out=g_tiles[q][:], in_=target_grad[:, q * width : (q + 1) * width])
+
+        def transpose_slots(words, slots):
+            bank = xt_pool.tile([P, SLOTS_PER_BANK, HALVES, P], F32, name="xt")
+            for s, t in enumerate(slots):
+                for u in range(HALVES):
+                    nc.tensor.transpose(bank[:, s, u, :], words[:, t, u : HALVES * P : HALVES], ident[:])
+            return bank
+
+        def words_view(tile_ap, slots):
+            return tile_ap.bitcast(F32).rearrange("q (t p u) -> q t p u", t=slots, u=HALVES)
+
+        def bank_source(bank, slots):
+            return bank[:, 0:slots].rearrange("q t u p -> q t p u")
+
+        def transpose_round(n):
+            banks = []
+            for c in range(n * ROUND, (n + 1) * ROUND):
+                words = raw[c][:].bitcast(F32)
+                for first in range(0, SLOTS, SLOTS_PER_BANK):
+                    banks.append((c, first, transpose_slots(words, range(first, first + SLOTS_PER_BANK))))
+            for c in range(n * ROUND, (n + 1) * ROUND):
+                grouped[c] = stage.tile([P, CHUNK * PACK], BF16, name="grouped", align_bytes=64)
+            for b, (c, first, bank) in enumerate(banks):
+                dst = words_view(grouped[c][:], SLOTS)[:, first : first + SLOTS_PER_BANK]
+                if b == len(banks) - 1:
+                    nc.vector.tensor_copy(out=dst, in_=bank_source(bank, SLOTS_PER_BANK))
+                else:
+                    nc.scalar.copy(out=dst, in_=bank_source(bank, SLOTS_PER_BANK))
+
+        def quantise_round(n):
+            for c in range(n * ROUND, (n + 1) * ROUND):
+                codes[c] = stage.tile([P, CHUNK], U32, name="codes", align_bytes=64)
+                scales[c] = stage.tile([P, CHUNK], U8, name="scales", align_bytes=64)
+                nc.vector.quantize_mx(
+                    out=codes[c][:].bitcast(FP8X4), scales=scales[c][:], in_=grouped[c][:]
+                )
+
+        def multiply_round(n):
+            for c in range(n * ROUND, (n + 1) * ROUND):
+                i = chunk_group[c]
+                acc[c] = acc_pool.tile([P, CHUNK], F32, name="acc")
+                nc.tensor.matmul_mx(
+                    out=acc[c][:],
+                    lhsT=e_codes[:, i, :].bitcast(FP8X4),
+                    lhsT_scale=e_scales[:, i, :],
+                    rhs=codes[c][:].bitcast(FP8X4),
+                    rhs_scale=scales[c][:],
+                    start=True,
+                    stop=True,
+                )
+
+        def subtract_round(n):
+            for h in range(ROUND):
+                c = n * ROUND + h
+                g_first = (n % G_ROUNDS) * round_cols + h * CHUNK
+                nc.vector.tensor_tensor(
+                    out=r_tiles[n][:, h * CHUNK : (h + 1) * CHUNK].rearrange("b (p t) -> b p t", t=SLOTS),
+                    in0=g_tiles[n // G_ROUNDS][:, g_first : g_first + CHUNK].rearrange(
+                        "b (p t) -> b p t", t=SLOTS
+                    ),
+                    in1=acc[c][:].rearrange("b (t p) -> b p t", t=SLOTS),
+                    op=ALU.subtract,
+                )
+
+        def square_round(n):
+            squares = stage.tile([P, round_cols], BF16, name="squares")
+            nc.scalar.activation(
+                out=squares[:], in_=r_tiles[n][:], func=ACT.Square, accum_out=sq_sums[:, n : n + 1]
+            )
+
+        load_round(0)
+        nc.sync.dma_start(out=e_sb[:], in_=embedding.rearrange("b (i k) -> b i k", k=K))
+        load_grad(0)
+        for n in range(1, AHEAD):
+            load_round(n)
+            load_grad(n)
+        make_identity(nc, ident[:])
+        nc.vector.memset(one[:], 1.0)
+        nc.vector.memset(out_cols[:], 0.0)
+        nc.scalar.activation(out=warm[:], in_=one[:], func=ACT.Sqrt)
+
+        transpose_round(0)
+        quantise_round(0)
+        e_words = e_sb[:].bitcast(F32)
+        for first in range(0, n_groups, SLOTS_PER_BANK):
+            slots = range(first, min(first + SLOTS_PER_BANK, n_groups))
+            bank = transpose_slots(e_words, slots)
+            nc.scalar.copy(
+                out=words_view(e_grouped[:], n_groups)[:, first : first + len(slots)],
+                in_=bank_source(bank, len(slots)),
+            )
+        for i in range(n_groups):
+            nc.vector.quantize_mx(
+                out=e_codes[:, i, :].bitcast(FP8X4),
+                scales=e_scales[:, i, :],
+                in_=e_grouped[:, i * P * PACK : (i + 1) * P * PACK],
+            )
+
+        for n in range(1, n_rounds + 2):
+            if n - 1 + AHEAD < n_rounds:
+                load_round(n - 1 + AHEAD)
+                load_grad(n - 1 + AHEAD)
+            if n < n_rounds:
+                transpose_round(n)
+            if n <= n_rounds:
+                multiply_round(n - 1)
+                subtract_round(n - 1)
+            if n < n_rounds:
+                quantise_round(n)
+            if n >= 2:
+                square_round(n - 2)
+
+        nc.vector.tensor_reduce(out=norm_sq[:], in_=sq_sums[:], axis=mybir.AxisListType.X, op=ALU.add)
+        nc.vector.tensor_scalar_max(out=floored[:], in0=norm_sq[:], scalar1=1.0)
+        nc.scalar.activation(out=norm_b[:], in_=floored[:], func=ACT.Sqrt, scale=float(P * P))
+        nc.vector.reciprocal(out=c_over_b[:], in_=norm_b[:])
+
+        def scale_round(n):
+            if n % PERIOD in (0, 3):
+                for h in range(ROUND):
+                    cols = r_tiles[n][:, h * CHUNK : (h + 1) * CHUNK]
+                    nc.scalar.activation(out=cols, in_=cols, func=ACT.Copy, scale=c_over_b[:])
+            else:
+                nc.gpsimd.tensor_scalar(
+                    out=r_tiles[n][:],
+                    in0=r_tiles[n][:],
+                    scalar1=c_over_b[:],
+                    scalar2=0.0,
+                    op0=ALU.mult,
+                    op1=ALU.add,
+                )
+
+        def sum_round(n):
+            for h in range(ROUND):
+                turned = xt_pool.tile([P, TILES_PER_BANK, P], F32, name="turned", tag="xt")
+                for s in range(TILES_PER_BANK):
+                    j = (h * TILES_PER_BANK + s) * P
+                    nc.tensor.transpose(turned[:, s, :], r_tiles[n][:, j : j + P], ident[:])
+                first = (n * ROUND + h) * TILES_PER_BANK
+                if n % PERIOD == 2:
+                    copied = stage.tile([P, TILES_PER_BANK, P], BF16, name="copied")
+                    for s in range(TILES_PER_BANK):
+                        nc.scalar.activation(
+                            out=copied[:, s, :],
+                            in_=turned[:, s, :],
+                            func=ACT.Copy,
+                            accum_out=out_cols[:, first + s : first + s + 1],
+                        )
+                else:
+                    nc.vector.tensor_reduce(
+                        out=out_cols[:, first : first + TILES_PER_BANK],
+                        in_=turned[:],
+                        axis=mybir.AxisListType.X,
+                        op=ALU.add,
+                    )
+
+        for n in range(LEAD):
+            scale_round(n)
+        for n in range(n_rounds):
+            if n + LEAD < n_rounds:
+                scale_round(n + LEAD)
+            sum_round(n)
+
+        flipped = acc_pool.tile([P, CHUNK], F32, name="flipped", tag="acc")
+        for h in range(2):
+            nc.tensor.transpose(flipped[:, h * P : (h + 1) * P], out_cols[:, h * P : (h + 1) * P], ident[:])
+        nc.vector.tensor_copy(out=out_rows[:], in_=flipped[:, 0 : 2 * P])
+        out_2d = out.rearrange("(m j) -> m j", j=P)
+        nc.sync.dma_start(out=out_2d[0:P, :], in_=out_rows[:, 0:P])
+        nc.scalar.dma_start(out=out_2d[P:n_col_tiles, :], in_=out_rows[0 : n_col_tiles - P, P : 2 * P])

@@ -23,6 +23,7 @@ G_ROUNDS = 2
 AHEAD = 3
 TILES_PER_BANK = 4
 PERIOD = 5
+SCALAR_SUMS = 4
 LEAD = 3
 
 FLOPS = 2 * 128 * 20480 * 512
@@ -61,7 +62,7 @@ def tile_gep_pb_kernel(tc, target_grad, embedding, bases0, bases1, bases2, out):
             for q in range(n_rounds // G_ROUNDS)
         ]
         r_tiles = [keep.tile([P, round_cols], F32, name="r%d" % n) for n in range(n_rounds)]
-        sq_sums = keep.tile([P, n_rounds], F32, name="sq_sums")
+        sq_sums = keep.tile([P, n_rounds - 1 + ROUND], F32, name="sq_sums")
         one = keep.tile([P, 1], F32, name="one")
         warm = keep.tile([P, 1], F32, name="warm")
         norm_sq = keep.tile([P, 1], F32, name="norm_sq")
@@ -80,9 +81,10 @@ def tile_gep_pb_kernel(tc, target_grad, embedding, bases0, bases1, bases2, out):
         def load_round(n):
             for c in range(n * ROUND, (n + 1) * ROUND):
                 raw[c] = raw_pool.tile([P, SLOTS, K], BF16, name="raw")
-                nc.sync.dma_start(
-                    out=raw[c][:], in_=chunk_rows[c].rearrange("(p t) k -> p t k", t=SLOTS)
-                )
+                rows = chunk_rows[c].rearrange("(p t) k -> p t k", t=SLOTS)
+                step = SLOTS_PER_BANK if c == 0 else SLOTS
+                for t in range(0, SLOTS, step):
+                    nc.sync.dma_start(out=raw[c][:, t : t + step], in_=rows[:, t : t + step])
 
         def load_grad(n):
             if n % G_ROUNDS == 0:
@@ -104,6 +106,12 @@ def tile_gep_pb_kernel(tc, target_grad, embedding, bases0, bases1, bases2, out):
             return bank[:, 0:slots].rearrange("q t u p -> q t p u")
 
         def transpose_round(n):
+            if n == 0:
+                vector_banks = (1, 3)
+            elif n % 4 == 3:
+                vector_banks = ()
+            else:
+                vector_banks = (3,)
             banks = []
             for c in range(n * ROUND, (n + 1) * ROUND):
                 words = raw[c][:].bitcast(F32)
@@ -113,7 +121,7 @@ def tile_gep_pb_kernel(tc, target_grad, embedding, bases0, bases1, bases2, out):
                 grouped[c] = stage.tile([P, CHUNK * PACK], BF16, name="grouped", align_bytes=64)
             for b, (c, first, bank) in enumerate(banks):
                 dst = words_view(grouped[c][:], SLOTS)[:, first : first + SLOTS_PER_BANK]
-                if b == len(banks) - 1:
+                if b in vector_banks:
                     nc.vector.tensor_copy(out=dst, in_=bank_source(bank, SLOTS_PER_BANK))
                 else:
                     nc.scalar.copy(out=dst, in_=bank_source(bank, SLOTS_PER_BANK))
@@ -154,10 +162,15 @@ def tile_gep_pb_kernel(tc, target_grad, embedding, bases0, bases1, bases2, out):
                 )
 
         def square_round(n):
-            squares = stage.tile([P, round_cols], BF16, name="squares")
-            nc.scalar.activation(
-                out=squares[:], in_=r_tiles[n][:], func=ACT.Square, accum_out=sq_sums[:, n : n + 1]
-            )
+            width = CHUNK if n == n_rounds - 1 else round_cols
+            for h in range(round_cols // width):
+                squares = stage.tile([P, round_cols], BF16, name="squares")
+                nc.scalar.activation(
+                    out=squares[:, 0:width],
+                    in_=r_tiles[n][:, h * width : (h + 1) * width],
+                    func=ACT.Square,
+                    accum_out=sq_sums[:, n + h : n + h + 1],
+                )
 
         load_round(0)
         nc.sync.dma_start(out=e_sb[:], in_=embedding.rearrange("b (i k) -> b i k", k=K))
@@ -206,11 +219,21 @@ def tile_gep_pb_kernel(tc, target_grad, embedding, bases0, bases1, bases2, out):
         nc.scalar.activation(out=norm_b[:], in_=floored[:], func=ACT.Sqrt, scale=float(P * P))
         nc.vector.reciprocal(out=c_over_b[:], in_=norm_b[:])
 
+        def scale_chunk(c, engine):
+            n, h = divmod(c, ROUND)
+            cols = r_tiles[n][:, h * CHUNK : (h + 1) * CHUNK]
+            if engine == "vector":
+                nc.vector.tensor_scalar_mul(out=cols, in0=cols, scalar1=c_over_b[:])
+            else:
+                nc.scalar.activation(out=cols, in_=cols, func=ACT.Copy, scale=c_over_b[:])
+
         def scale_round(n):
-            if n % PERIOD in (0, 3):
+            if n == 0:
+                scale_chunk(0, "vector")
+                scale_chunk(1, "scalar")
+            elif n % PERIOD in (0, 3):
                 for h in range(ROUND):
-                    cols = r_tiles[n][:, h * CHUNK : (h + 1) * CHUNK]
-                    nc.scalar.activation(out=cols, in_=cols, func=ACT.Copy, scale=c_over_b[:])
+                    scale_chunk(n * ROUND + h, "scalar")
             else:
                 nc.gpsimd.tensor_scalar(
                     out=r_tiles[n][:],
@@ -221,41 +244,48 @@ def tile_gep_pb_kernel(tc, target_grad, embedding, bases0, bases1, bases2, out):
                     op1=ALU.add,
                 )
 
-        def sum_round(n):
-            for h in range(ROUND):
-                turned = xt_pool.tile([P, TILES_PER_BANK, P], F32, name="turned", tag="xt")
+        def sum_chunk(c):
+            n, h = divmod(c, ROUND)
+            turned = xt_pool.tile([P, TILES_PER_BANK, P], F32, name="turned", tag="xt")
+            for s in range(TILES_PER_BANK):
+                j = (h * TILES_PER_BANK + s) * P
+                nc.tensor.transpose(turned[:, s, :], r_tiles[n][:, j : j + P], ident[:])
+            first = c * TILES_PER_BANK
+            if c % SCALAR_SUMS == SCALAR_SUMS - 1:
+                copied = stage.tile([P, TILES_PER_BANK, P], BF16, name="copied")
                 for s in range(TILES_PER_BANK):
-                    j = (h * TILES_PER_BANK + s) * P
-                    nc.tensor.transpose(turned[:, s, :], r_tiles[n][:, j : j + P], ident[:])
-                first = (n * ROUND + h) * TILES_PER_BANK
-                if n % PERIOD == 2:
-                    copied = stage.tile([P, TILES_PER_BANK, P], BF16, name="copied")
-                    for s in range(TILES_PER_BANK):
-                        nc.scalar.activation(
-                            out=copied[:, s, :],
-                            in_=turned[:, s, :],
-                            func=ACT.Copy,
-                            accum_out=out_cols[:, first + s : first + s + 1],
-                        )
-                else:
-                    nc.vector.tensor_reduce(
-                        out=out_cols[:, first : first + TILES_PER_BANK],
-                        in_=turned[:],
-                        axis=mybir.AxisListType.X,
-                        op=ALU.add,
+                    nc.scalar.activation(
+                        out=copied[:, s, :],
+                        in_=turned[:, s, :],
+                        func=ACT.Copy,
+                        accum_out=out_cols[:, first + s : first + s + 1],
                     )
+            else:
+                nc.vector.tensor_reduce(
+                    out=out_cols[:, first : first + TILES_PER_BANK],
+                    in_=turned[:],
+                    axis=mybir.AxisListType.X,
+                    op=ALU.add,
+                )
 
+        out_2d = out.rearrange("(m j) -> m j", j=P)
+
+        def store_half(h):
+            flipped = acc_pool.tile([P, CHUNK], F32, name="flipped", tag="acc")
+            nc.tensor.transpose(flipped[:, 0:P], out_cols[:, h * P : (h + 1) * P], ident[:])
+            rows = min(P, n_col_tiles - h * P)
+            nc.vector.tensor_copy(out=out_rows[:, h * P : (h + 1) * P], in_=flipped[:, 0:P])
+            nc.sync.dma_start(
+                out=out_2d[h * P : h * P + rows, :], in_=out_rows[0:rows, h * P : (h + 1) * P]
+            )
+
+        n_chunks = len(chunk_rows)
         for n in range(LEAD):
             scale_round(n)
-        for n in range(n_rounds):
-            if n + LEAD < n_rounds:
-                scale_round(n + LEAD)
-            sum_round(n)
-
-        flipped = acc_pool.tile([P, CHUNK], F32, name="flipped", tag="acc")
-        for h in range(2):
-            nc.tensor.transpose(flipped[:, h * P : (h + 1) * P], out_cols[:, h * P : (h + 1) * P], ident[:])
-        nc.vector.tensor_copy(out=out_rows[:], in_=flipped[:, 0 : 2 * P])
-        out_2d = out.rearrange("(m j) -> m j", j=P)
-        nc.sync.dma_start(out=out_2d[0:P, :], in_=out_rows[:, 0:P])
-        nc.scalar.dma_start(out=out_2d[P:n_col_tiles, :], in_=out_rows[0 : n_col_tiles - P, P : 2 * P])
+        for c in range(n_chunks):
+            if c % ROUND == 0 and c // ROUND + LEAD < n_rounds:
+                scale_round(c // ROUND + LEAD)
+            sum_chunk(c)
+            if c == P // TILES_PER_BANK + 3:
+                store_half(0)
+        store_half(1)

@@ -106,12 +106,7 @@ def tile_gep_pb_kernel(tc, target_grad, embedding, bases0, bases1, bases2, out):
             return bank[:, 0:slots].rearrange("q t u p -> q t p u")
 
         def transpose_round(n):
-            if n == 0:
-                vector_banks = (1, 3)
-            elif n % 4 == 3:
-                vector_banks = ()
-            else:
-                vector_banks = (3,)
+            vector_banks = (1, 3) if n == 0 else (0,)
             banks = []
             for c in range(n * ROUND, (n + 1) * ROUND):
                 words = raw[c][:].bitcast(F32)

@@ -22,8 +22,12 @@ ROUND = 2
 G_ROUNDS = 2
 AHEAD = 3
 TILES_PER_BANK = 4
-PERIOD = 5
+SCALAR_SCALES = 3
 SCALAR_SUMS = 4
+PIECES = 4
+PIECE = ROUND * CHUNK // PIECES
+PIECE_EVERY = 9
+PIECE_FIRST = 5
 LEAD = 3
 
 FLOPS = 2 * 128 * 20480 * 512
@@ -42,7 +46,6 @@ def tile_gep_pb_kernel(tc, target_grad, embedding, bases0, bases1, bases2, out):
             chunk_rows.append(bases[first : first + CHUNK, :])
     n_rounds = len(chunk_rows) // ROUND
     round_cols = ROUND * CHUNK
-    n_col_tiles = n_rounds * round_cols // P
 
     with ExitStack() as stack:
         keep = stack.enter_context(tc.tile_pool(name="keep", bufs=1))
@@ -65,12 +68,14 @@ def tile_gep_pb_kernel(tc, target_grad, embedding, bases0, bases1, bases2, out):
         sq_sums = keep.tile([P, n_rounds - 1 + ROUND], F32, name="sq_sums")
         one = keep.tile([P, 1], F32, name="one")
         warm = keep.tile([P, 1], F32, name="warm")
-        norm_sq = keep.tile([P, 1], F32, name="norm_sq")
+        norm_part = keep.tile([P, 1], F32, name="norm_part")
         floored = keep.tile([P, 1], F32, name="floored")
         norm_b = keep.tile([P, 1], F32, name="norm_b")
-        c_over_b = keep.tile([P, 1], F32, name="c_over_b")
+        window = keep.tile([P, 2 * P - 1], F32, name="window")
+        c_over_b = window[:, P - 1 : P]
         out_cols = keep.tile([P, 2 * P], F32, name="out_cols")
         out_rows = keep.tile([P, 2 * P], F32, name="out_rows")
+        last_rows = keep.tile([P, PIECE], F32, name="last_rows")
 
         raw = {}
         grouped = {}
@@ -87,7 +92,7 @@ def tile_gep_pb_kernel(tc, target_grad, embedding, bases0, bases1, bases2, out):
                     nc.sync.dma_start(out=raw[c][:, t : t + step], in_=rows[:, t : t + step])
 
         def load_grad(n):
-            if n % G_ROUNDS == 0:
+            if n % G_ROUNDS == G_ROUNDS - 1:
                 q = n // G_ROUNDS
                 width = G_ROUNDS * round_cols
                 nc.sync.dma_start(out=g_tiles[q][:], in_=target_grad[:, q * width : (q + 1) * width])
@@ -164,6 +169,7 @@ def tile_gep_pb_kernel(tc, target_grad, embedding, bases0, bases1, bases2, out):
                     out=squares[:, 0:width],
                     in_=r_tiles[n][:, h * width : (h + 1) * width],
                     func=ACT.Square,
+                    scale=float(P),
                     accum_out=sq_sums[:, n + h : n + h + 1],
                 )
 
@@ -176,6 +182,7 @@ def tile_gep_pb_kernel(tc, target_grad, embedding, bases0, bases1, bases2, out):
         make_identity(nc, ident[:])
         nc.vector.memset(one[:], 1.0)
         nc.vector.memset(out_cols[:], 0.0)
+        nc.gpsimd.memset(window[:], 0.0)
         nc.scalar.activation(out=warm[:], in_=one[:], func=ACT.Sqrt)
 
         transpose_round(0)
@@ -209,31 +216,40 @@ def tile_gep_pb_kernel(tc, target_grad, embedding, bases0, bases1, bases2, out):
             if n >= 2:
                 square_round(n - 2)
 
-        nc.vector.tensor_reduce(out=norm_sq[:], in_=sq_sums[:], axis=mybir.AxisListType.X, op=ALU.add)
-        nc.vector.tensor_scalar_max(out=floored[:], in0=norm_sq[:], scalar1=1.0)
-        nc.scalar.activation(out=norm_b[:], in_=floored[:], func=ACT.Sqrt, scale=float(P * P))
-        nc.vector.reciprocal(out=c_over_b[:], in_=norm_b[:])
+        nc.vector.tensor_reduce(
+            out=norm_part[:], in_=sq_sums[:, 0:n_rounds], axis=mybir.AxisListType.X, op=ALU.add
+        )
+        nc.vector.tensor_scalar(
+            out=floored[:],
+            in0=sq_sums[:, n_rounds : n_rounds + 1],
+            scalar1=norm_part[:],
+            scalar2=float(P * P),
+            op0=ALU.add,
+            op1=ALU.max,
+        )
+        nc.scalar.activation(out=norm_b[:], in_=floored[:], func=ACT.Sqrt)
+        nc.vector.reciprocal(out=c_over_b, in_=norm_b[:])
 
         def scale_chunk(c, engine):
             n, h = divmod(c, ROUND)
             cols = r_tiles[n][:, h * CHUNK : (h + 1) * CHUNK]
             if engine == "vector":
-                nc.vector.tensor_scalar_mul(out=cols, in0=cols, scalar1=c_over_b[:])
+                nc.vector.tensor_scalar_mul(out=cols, in0=cols, scalar1=c_over_b)
             else:
-                nc.scalar.activation(out=cols, in_=cols, func=ACT.Copy, scale=c_over_b[:])
+                nc.scalar.activation(out=cols, in_=cols, func=ACT.Copy, scale=c_over_b)
 
         def scale_round(n):
             if n == 0:
                 scale_chunk(0, "vector")
                 scale_chunk(1, "scalar")
-            elif n % PERIOD in (0, 3):
+            elif n % SCALAR_SCALES == 1:
                 for h in range(ROUND):
                     scale_chunk(n * ROUND + h, "scalar")
             else:
                 nc.gpsimd.tensor_scalar(
                     out=r_tiles[n][:],
                     in0=r_tiles[n][:],
-                    scalar1=c_over_b[:],
+                    scalar1=c_over_b,
                     scalar2=0.0,
                     op0=ALU.mult,
                     op1=ALU.add,
@@ -246,7 +262,7 @@ def tile_gep_pb_kernel(tc, target_grad, embedding, bases0, bases1, bases2, out):
                 j = (h * TILES_PER_BANK + s) * P
                 nc.tensor.transpose(turned[:, s, :], r_tiles[n][:, j : j + P], ident[:])
             first = c * TILES_PER_BANK
-            if c % SCALAR_SUMS == SCALAR_SUMS - 1:
+            if c % SCALAR_SUMS == 1:
                 copied = stage.tile([P, TILES_PER_BANK, P], BF16, name="copied")
                 for s in range(TILES_PER_BANK):
                     nc.scalar.activation(
@@ -268,19 +284,35 @@ def tile_gep_pb_kernel(tc, target_grad, embedding, bases0, bases1, bases2, out):
         def store_half(h):
             flipped = acc_pool.tile([P, CHUNK], F32, name="flipped", tag="acc")
             nc.tensor.transpose(flipped[:, 0:P], out_cols[:, h * P : (h + 1) * P], ident[:])
-            rows = min(P, n_col_tiles - h * P)
+            rows = min(P, n_turned * round_cols // P - h * P)
             nc.vector.tensor_copy(out=out_rows[:, h * P : (h + 1) * P], in_=flipped[:, 0:P])
             nc.sync.dma_start(
                 out=out_2d[h * P : h * P + rows, :], in_=out_rows[0:rows, h * P : (h + 1) * P]
             )
 
-        n_chunks = len(chunk_rows)
+        n_turned = n_rounds - 1
+        last_sums = acc_pool.tile([P, CHUNK], F32, name="last_sums", tag="acc")
         for n in range(LEAD):
             scale_round(n)
-        for c in range(n_chunks):
-            if c % ROUND == 0 and c // ROUND + LEAD < n_rounds:
+        for c in range(n_turned * ROUND):
+            if c % ROUND == 0 and c // ROUND + LEAD < n_turned:
                 scale_round(c // ROUND + LEAD)
             sum_chunk(c)
-            if c == P // TILES_PER_BANK + 3:
+            if c == n_turned * ROUND - 4:
                 store_half(0)
+            if c % PIECE_EVERY == PIECE_FIRST:
+                m = c // PIECE_EVERY
+                nc.tensor.matmul(
+                    out=last_sums[:, 0:PIECE],
+                    lhsT=window[:, P - 1 - m : 2 * P - 1 - m],
+                    rhs=r_tiles[n_rounds - 1][:, m * PIECE : (m + 1) * PIECE],
+                    start=(m == 0),
+                    stop=(m == PIECES - 1),
+                )
+                if m == PIECES - 1:
+                    nc.scalar.copy(out=last_rows[0:32, :], in_=last_sums[0:32, 0:PIECE])
+                    nc.scalar.dma_start(
+                        out=out[n_turned * round_cols :].rearrange("(m x) -> m x", x=PIECE),
+                        in_=last_rows[0:PIECES, :],
+                    )
         store_half(1)

from contextlib import ExitStack

import concourse.mybir as mybir
from concourse.masks import make_identity

F32 = mybir.dt.float32
BF16 = mybir.dt.bfloat16
U32 = mybir.dt.uint32
U8 = mybir.dt.uint8
FP8X4 = mybir.dt.float8_e4m3fn_x4
ALU = mybir.AluOpType
ACT = mybir.ActivationFunctionType

P = 128
K = 512
PACK = 4
HALVES = 2
SLOTS = 4
CHUNK = P * SLOTS
SLOTS_PER_BANK = 2
ROUND = 2
G_ROUNDS = 2
AHEAD = 3
TILES_PER_BANK = 4
SCALAR_SCALES = 3
SCALAR_SUMS = 4
PIECES = 4
PIECE = ROUND * CHUNK // PIECES
PIECE_EVERY = 9
PIECE_FIRST = 5
LEAD = 3

FLOPS = 2 * 128 * 20480 * 512


def tile_gep_pb_kernel(tc, target_grad, embedding, bases0, bases1, bases2, out):
    nc = tc.nc
    groups = (bases0, bases1, bases2)
    n_groups = len(groups)

    chunk_group = []
    chunk_rows = []
    for i, bases in enumerate(groups):
        for first in range(0, bases.shape[0], CHUNK):
            chunk_group.append(i)
            chunk_rows.append(bases[first : first + CHUNK, :])
    n_rounds = len(chunk_rows) // ROUND
    round_cols = ROUND * CHUNK

    with ExitStack() as stack:
        keep = stack.enter_context(tc.tile_pool(name="keep", bufs=1))
        raw_pool = stack.enter_context(tc.tile_pool(name="raw_pool", bufs=(AHEAD + 1) * ROUND))
        stage = stack.enter_context(tc.tile_pool(name="stage", bufs=2 * ROUND))
        xt_pool = stack.enter_context(tc.psum_pool(name="xt_pool", bufs=6))
        acc_pool = stack.enter_context(tc.psum_pool(name="acc_pool", bufs=ROUND))
        stack.enter_context(tc.manual_schedule())

        ident = keep.tile([P, P], F32, name="ident")
        e_sb = keep.tile([P, n_groups, K], BF16, name="e_sb")
        e_grouped = keep.tile([P, n_groups * P * PACK], BF16, name="e_grouped", align_bytes=64)
        e_codes = keep.tile([P, n_groups, P], U32, name="e_codes", align_bytes=64)
        e_scales = keep.tile([P, n_groups, P], U8, name="e_scales", align_bytes=64)
        g_tiles = [
            keep.tile([P, G_ROUNDS * round_cols], BF16, name="g%d" % q)
            for q in range(n_rounds // G_ROUNDS)
        ]
        r_tiles = [keep.tile([P, round_cols], F32, name="r%d" % n) for n in range(n_rounds)]
        sq_sums = keep.tile([P, n_rounds - 1 + ROUND], F32, name="sq_sums")
        one = keep.tile([P, 1], F32, name="one")
        warm = keep.tile([P, 1], F32, name="warm")
        norm_part = keep.tile([P, 1], F32, name="norm_part")
        floored = keep.tile([P, 1], F32, name="floored")
        norm_b = keep.tile([P, 1], F32, name="norm_b")
        window = keep.tile([P, 2 * P - 1], F32, name="window")
        c_over_b = window[:, P - 1 : P]
        out_cols = keep.tile([P, 2 * P], F32, name="out_cols")
        out_rows = keep.tile([P, 2 * P], F32, name="out_rows")
        last_rows = keep.tile([P, PIECE], F32, name="last_rows")

        raw = {}
        grouped = {}
        codes = {}
        scales = {}
        acc = {}

        def load_round(n):
            for c in range(n * ROUND, (n + 1) * ROUND):
                raw[c] = raw_pool.tile([P, SLOTS, K], BF16, name="raw")
                rows = chunk_rows[c].rearrange("(p t) k -> p t k", t=SLOTS)
                step = SLOTS_PER_BANK if c == 0 else SLOTS
                for t in range(0, SLOTS, step):
                    nc.sync.dma_start(out=raw[c][:, t : t + step], in_=rows[:, t : t + step])

        def load_grad(n):
            if n % G_ROUNDS == G_ROUNDS - 1:
                q = n // G_ROUNDS
                width = G_ROUNDS * round_cols
                nc.sync.dma_start(out=g_tiles[q][:], in_=target_grad[:, q * width : (q + 1) * width])

        def transpose_slots(words, slots):
            bank = xt_pool.tile([P, SLOTS_PER_BANK, HALVES, P], F32, name="xt")
            for s, t in enumerate(slots):
                for u in range(HALVES):
                    nc.tensor.transpose(bank[:, s, u, :], words[:, t, u : HALVES * P : HALVES], ident[:])
            return bank

        def words_view(tile_ap, slots):
            return tile_ap.bitcast(F32).rearrange("q (t p u) -> q t p u", t=slots, u=HALVES)

        def bank_source(bank, slots):
            return bank[:, 0:slots].rearrange("q t u p -> q t p u")

        def transpose_round(n):
            vector_banks = (1, 3) if n == 0 else (0,)
            banks = []
            for c in range(n * ROUND, (n + 1) * ROUND):
                words = raw[c][:].bitcast(F32)
                for first in range(0, SLOTS, SLOTS_PER_BANK):
                    banks.append((c, first, transpose_slots(words, range(first, first + SLOTS_PER_BANK))))
            for c in range(n * ROUND, (n + 1) * ROUND):
                grouped[c] = stage.tile([P, CHUNK * PACK], BF16, name="grouped", align_bytes=64)
            for b, (c, first, bank) in enumerate(banks):
                dst = words_view(grouped[c][:], SLOTS)[:, first : first + SLOTS_PER_BANK]
                if b in vector_banks:
                    nc.vector.tensor_copy(out=dst, in_=bank_source(bank, SLOTS_PER_BANK))
                else:
                    nc.scalar.copy(out=dst, in_=bank_source(bank, SLOTS_PER_BANK))

        def quantise_round(n):
            for c in range(n * ROUND, (n + 1) * ROUND):
                codes[c] = stage.tile([P, CHUNK], U32, name="codes", align_bytes=64)
                scales[c] = stage.tile([P, CHUNK], U8, name="scales", align_bytes=64)
                nc.vector.quantize_mx(
                    out=codes[c][:].bitcast(FP8X4), scales=scales[c][:], in_=grouped[c][:]
                )

        def multiply_round(n):
            for c in range(n * ROUND, (n + 1) * ROUND):
                i = chunk_group[c]
                acc[c] = acc_pool.tile([P, CHUNK], F32, name="acc")
                nc.tensor.matmul_mx(
                    out=acc[c][:],
                    lhsT=e_codes[:, i, :].bitcast(FP8X4),
                    lhsT_scale=e_scales[:, i, :],
                    rhs=codes[c][:].bitcast(FP8X4),
                    rhs_scale=scales[c][:],
                    start=True,
                    stop=True,
                )

        def subtract_round(n):
            for h in range(ROUND):
                c = n * ROUND + h
                g_first = (n % G_ROUNDS) * round_cols + h * CHUNK
                nc.vector.tensor_tensor(
                    out=r_tiles[n][:, h * CHUNK : (h + 1) * CHUNK].rearrange("b (p t) -> b p t", t=SLOTS),
                    in0=g_tiles[n // G_ROUNDS][:, g_first : g_first + CHUNK].rearrange(
                        "b (p t) -> b p t", t=SLOTS
                    ),
                    in1=acc[c][:].rearrange("b (t p) -> b p t", t=SLOTS),
                    op=ALU.subtract,
                )

        def square_round(n):
            width = CHUNK if n == n_rounds - 1 else round_cols
            for h in range(round_cols // width):
                squares = stage.tile([P, round_cols], BF16, name="squares")
                nc.scalar.activation(
                    out=squares[:, 0:width],
                    in_=r_tiles[n][:, h * width : (h + 1) * width],
                    func=ACT.Square,
                    scale=float(P),
                    accum_out=sq_sums[:, n + h : n + h + 1],
                )

        load_round(0)
        nc.sync.dma_start(out=e_sb[:], in_=embedding.rearrange("b (i k) -> b i k", k=K))
        load_grad(0)
        for n in range(1, AHEAD):
            load_round(n)
            load_grad(n)
        make_identity(nc, ident[:])
        nc.vector.memset(one[:], 1.0)
        nc.vector.memset(out_cols[:], 0.0)
        nc.gpsimd.memset(window[:], 0.0)
        nc.scalar.activation(out=warm[:], in_=one[:], func=ACT.Sqrt)

        transpose_round(0)
        quantise_round(0)
        e_words = e_sb[:].bitcast(F32)
        for first in range(0, n_groups, SLOTS_PER_BANK):
            slots = range(first, min(first + SLOTS_PER_BANK, n_groups))
            bank = transpose_slots(e_words, slots)
            nc.scalar.copy(
                out=words_view(e_grouped[:], n_groups)[:, first : first + len(slots)],
                in_=bank_source(bank, len(slots)),
            )
        for i in range(n_groups):
            nc.vector.quantize_mx(
                out=e_codes[:, i, :].bitcast(FP8X4),
                scales=e_scales[:, i, :],
                in_=e_grouped[:, i * P * PACK : (i + 1) * P * PACK],
            )

        for n in range(1, n_rounds + 2):
            if n - 1 + AHEAD < n_rounds:
                load_round(n - 1 + AHEAD)
                load_grad(n - 1 + AHEAD)
            if n < n_rounds:
                transpose_round(n)
            if n <= n_rounds:
                multiply_round(n - 1)
                subtract_round(n - 1)
            if n < n_rounds:
                quantise_round(n)
            if n >= 2:
                square_round(n - 2)

        nc.vector.tensor_reduce(
            out=norm_part[:], in_=sq_sums[:, 0:n_rounds], axis=mybir.AxisListType.X, op=ALU.add
        )
        nc.vector.tensor_scalar(
            out=floored[:],
            in0=sq_sums[:, n_rounds : n_rounds + 1],
            scalar1=norm_part[:],
            scalar2=float(P * P),
            op0=ALU.add,
            op1=ALU.max,
        )
        nc.scalar.activation(out=norm_b[:], in_=floored[:], func=ACT.Sqrt)
        nc.vector.reciprocal(out=c_over_b, in_=norm_b[:])

        def scale_chunk(c, engine):
            n, h = divmod(c, ROUND)
            cols = r_tiles[n][:, h * CHUNK : (h + 1) * CHUNK]
            if engine == "vector":
                nc.vector.tensor_scalar_mul(out=cols, in0=cols, scalar1=c_over_b)
            else:
                nc.scalar.activation(out=cols, in_=cols, func=ACT.Copy, scale=c_over_b)

        def scale_round(n):
            if n == 0:
                scale_chunk(0, "vector")
                scale_chunk(1, "scalar")
            elif n % SCALAR_SCALES == 1:
                for h in range(ROUND):
                    scale_chunk(n * ROUND + h, "scalar")
            else:
                nc.gpsimd.tensor_scalar(
                    out=r_tiles[n][:],
                    in0=r_tiles[n][:],
                    scalar1=c_over_b,
                    scalar2=0.0,
                    op0=ALU.mult,
                    op1=ALU.add,
                )

        def sum_chunk(c):
            n, h = divmod(c, ROUND)
            turned = xt_pool.tile([P, TILES_PER_BANK, P], F32, name="turned", tag="xt")
            for s in range(TILES_PER_BANK):
                j = (h * TILES_PER_BANK + s) * P
                nc.tensor.transpose(turned[:, s, :], r_tiles[n][:, j : j + P], ident[:])
            first = c * TILES_PER_BANK
            if c % SCALAR_SUMS == 1:
                copied = stage.tile([P, TILES_PER_BANK, P], BF16, name="copied")
                for s in range(TILES_PER_BANK):
                    nc.scalar.activation(
                        out=copied[:, s, :],
                        in_=turned[:, s, :],
                        func=ACT.Copy,
                        accum_out=out_cols[:, first + s : first + s + 1],
                    )
            else:
                nc.vector.tensor_reduce(
                    out=out_cols[:, first : first + TILES_PER_BANK],
                    in_=turned[:],
                    axis=mybir.AxisListType.X,
                    op=ALU.add,
                )

        out_2d = out.rearrange("(m j) -> m j", j=P)

        def store_half(h):
            flipped = acc_pool.tile([P, CHUNK], F32, name="flipped", tag="acc")
            nc.tensor.transpose(flipped[:, 0:P], out_cols[:, h * P : (h + 1) * P], ident[:])
            rows = min(P, n_turned * round_cols // P - h * P)
            nc.vector.tensor_copy(out=out_rows[:, h * P : (h + 1) * P], in_=flipped[:, 0:P])
            nc.sync.dma_start(
                out=out_2d[h * P : h * P + rows, :], in_=out_rows[0:rows, h * P : (h + 1) * P]
            )

        n_turned = n_rounds - 1
        last_sums = acc_pool.tile([P, CHUNK], F32, name="last_sums", tag="acc")
        for n in range(LEAD):
            scale_round(n)
        for c in range(n_turned * ROUND):
            if c % ROUND == 0 and c // ROUND + LEAD < n_turned:
                scale_round(c // ROUND + LEAD)
            sum_chunk(c)
            if c == n_turned * ROUND - 4:
                store_half(0)
            if c % PIECE_EVERY == PIECE_FIRST:
                m = c // PIECE_EVERY
                nc.tensor.matmul(
                    out=last_sums[:, 0:PIECE],
                    lhsT=window[:, P - 1 - m : 2 * P - 1 - m],
                    rhs=r_tiles[n_rounds - 1][:, m * PIECE : (m + 1) * PIECE],
                    start=(m == 0),
                    stop=(m == PIECES - 1),
                )
                if m == PIECES - 1:
                    nc.scalar.copy(out=last_rows[0:32, :], in_=last_sums[0:32, 0:PIECE])
                    nc.scalar.dma_start(
                        out=out[n_turned * round_cols :].rearrange("(m x) -> m x", x=PIECE),
                        in_=last_rows[0:PIECES, :],
                    )
        store_half(1)
